import numpy as np
import ml_dtypes

BF16 = ml_dtypes.bfloat16


def bf(x):
    return np.asarray(x, np.float32).astype(BF16)


def f32(x):
    return np.asarray(x, np.float32)


def f64(x):
    return np.asarray(x).astype(np.float64)


def striped(idx):
    return np.tile(idx.reshape(-1, 16).T, (8, 1))


S, D, M, N = 1024, 128, 512, 1024


def setup_inputs():
    return {"table": bf(np.random.standard_normal((S, D))), "w": bf(np.random.standard_normal((D, M))), "offs": striped(np.random.permutation(S)[:N])}


def reference(table, w, offs):
    idx = offs[:16].T.reshape(-1)
    x = f64(table)
    y = f64(w)
    xh = x / np.sqrt((x * x).sum(axis=1, keepdims=True))
    yn = np.sqrt((y * y).sum(axis=0))[:, None]
    return 1.0 - (y.T @ xh[idx].T) / yn

@@ -1,0 +1,95 @@
+import concourse.mybir as mybir
+from concourse.masks import make_identity
+
+BF16, F32, U16 = mybir.dt.bfloat16, mybir.dt.float32, mybir.dt.uint16
+MULT, ADD = mybir.AluOpType.mult, mybir.AluOpType.add
+SQRT, COPY = mybir.ActivationFunctionType.Sqrt, mybir.ActivationFunctionType.Copy
+
+P = 128
+S, D, M, N = 1024, 128, 512, 1024
+S_BLOCKS = S // P
+M_BLOCKS = M // P
+PIECE = 512
+PIECES = N // PIECE
+PIECE_COLUMNS = PIECE // 16
+
+FLOPS = 2 * M * N * D
+
+
+def tile_optimaltransportloss_kernel(tc, table, w, offs, out):
+    nc = tc.nc
+    with (
+        tc.tile_pool(name="held", bufs=1) as held,
+        tc.tile_pool(name="staged", bufs=4) as staged,
+        tc.psum_pool(name="once", bufs=1) as once,
+        tc.psum_pool(name="banks", bufs=4) as banks,
+    ):
+        offsets = held.tile([P, N // 16], U16, name="offsets")
+        nc.sync.dma_start(offsets[:], offs)
+        rows = held.tile([P, S_BLOCKS, D], BF16, name="rows")
+        nc.sync.dma_start(rows[:], table.rearrange("(b p) d -> p b d", p=P))
+        targets = held.tile([D, M], BF16, name="targets")
+        nc.scalar.dma_start(targets[:], w)
+
+        identity = held.tile([P, P], BF16, name="identity")
+        make_identity(nc, identity[:])
+        ones = held.tile([D, 1], F32, name="ones")
+        nc.vector.memset(ones[:], 1.0)
+
+        row_squares = held.tile([P, S_BLOCKS, D], F32, name="row_squares")
+        nc.vector.tensor_tensor(row_squares[:], rows[:], rows[:], MULT)
+        row_sums = held.tile([P, S_BLOCKS], F32, name="row_sums")
+        nc.vector.tensor_reduce(row_sums[:], row_squares[:], mybir.AxisListType.X, ADD)
+        row_norms = held.tile([P, S_BLOCKS], F32, name="row_norms")
+        nc.scalar.activation(row_norms[:], row_sums[:], SQRT)
+        row_scales = held.tile([P, S_BLOCKS], F32, name="row_scales")
+        nc.vector.reciprocal(row_scales[:], row_norms[:])
+
+        unit_rows = held.tile([P, S_BLOCKS, D], BF16, name="unit_rows")
+        flipped = once.tile([D, S], BF16, name="flipped")
+        for b in range(S_BLOCKS):
+            nc.vector.tensor_scalar(
+                unit_rows[:, b, :], rows[:, b, :], row_scales[:, b : b + 1], None, op0=MULT
+            )
+            nc.tensor.transpose(flipped[:, b * P : (b + 1) * P], unit_rows[:, b, :], identity[:])
+        window = held.tile([D, S], BF16, name="window")
+        nc.vector.tensor_copy(window[:], flipped[:])
+
+        target_squares = held.tile([D, M], F32, name="target_squares")
+        nc.gpsimd.tensor_tensor(target_squares[:], targets[:], targets[:], MULT)
+        target_sums = once.tile([P, M_BLOCKS], F32, name="target_sums")
+        for mb in range(M_BLOCKS):
+            nc.tensor.matmul(
+                target_sums[:, mb : mb + 1],
+                target_squares[:, mb * P : (mb + 1) * P],
+                ones[:],
+                start=True,
+                stop=True,
+            )
+        target_norms = held.tile([P, M_BLOCKS], F32, name="target_norms")
+        nc.scalar.activation(target_norms[:], target_sums[:], SQRT)
+        target_scales = held.tile([P, M_BLOCKS], F32, name="target_scales")
+        nc.vector.reciprocal(target_scales[:], target_norms[:])
+        minus_scales = held.tile([P, M_BLOCKS], F32, name="minus_scales")
+        nc.vector.tensor_scalar(minus_scales[:], target_scales[:], -1.0, None, op0=MULT)
+
+        for mb in range(M_BLOCKS):
+            for piece in range(PIECES):
+                looked_up = window[:].indirect(
+                    offsets[:, piece * PIECE_COLUMNS : (piece + 1) * PIECE_COLUMNS]
+                )
+                product = banks.tile([P, PIECE], F32, name="product")
+                nc.tensor.matmul(
+                    product[:], targets[:, mb * P : (mb + 1) * P], looked_up, start=True, stop=True
+                )
+                distance = staged.tile([P, PIECE], F32, name="distance")
+                minus_scale = minus_scales[:, mb : mb + 1]
+                if piece % 2 == 0:
+                    nc.vector.tensor_scalar(
+                        distance[:], product[:], minus_scale, 1.0, op0=MULT, op1=ADD
+                    )
+                else:
+                    nc.scalar.activation(distance[:], product[:], COPY, bias=1.0, scale=minus_scale)
+                nc.sync.dma_start(
+                    out[mb * P : (mb + 1) * P, piece * PIECE : (piece + 1) * PIECE], distance[:]
+                )

@@ -3,11 +3,15 @@ from concourse.masks import make_identity
 
 BF16, F32, U16 = mybir.dt.bfloat16, mybir.dt.float32, mybir.dt.uint16
 MULT, ADD = mybir.AluOpType.mult, mybir.AluOpType.add
-SQRT, COPY = mybir.ActivationFunctionType.Sqrt, mybir.ActivationFunctionType.Copy
+SQRT = mybir.ActivationFunctionType.Sqrt
+SQUARE = mybir.ActivationFunctionType.Square
+COPY = mybir.ActivationFunctionType.Copy
 
 P = 128
 S, D, M, N = 1024, 128, 512, 1024
-S_BLOCKS = S // P
+HALVES = 2
+HALF = S // HALVES
+HALF_BLOCKS = HALF // P
 M_BLOCKS = M // P
 PIECE = 512
 PIECES = N // PIECE
@@ -20,40 +24,23 @@ def tile_optimaltransportloss_kernel(tc, table, w, offs, out):
     nc = tc.nc
     with (
         tc.tile_pool(name="held", bufs=1) as held,
-        tc.tile_pool(name="staged", bufs=4) as staged,
+        tc.tile_pool(name="staged", bufs=M_BLOCKS * PIECES) as staged,
         tc.psum_pool(name="once", bufs=1) as once,
-        tc.psum_pool(name="banks", bufs=4) as banks,
+        tc.psum_pool(name="banks", bufs=5) as banks,
     ):
+        table_halves = table.rearrange("(h k p) d -> h p k d", h=HALVES, p=P)
+        rows = [held.tile([P, HALF_BLOCKS, D], BF16, name=f"rows{h}") for h in range(HALVES)]
+        nc.scalar.dma_start(rows[0][:], table_halves[0])
+        nc.sync.dma_start(rows[1][:], table_halves[1])
+        targets = held.tile([D, M], BF16, name="targets")
+        nc.sync.dma_start(targets[:], w)
         offsets = held.tile([P, N // 16], U16, name="offsets")
         nc.sync.dma_start(offsets[:], offs)
-        rows = held.tile([P, S_BLOCKS, D], BF16, name="rows")
-        nc.sync.dma_start(rows[:], table.rearrange("(b p) d -> p b d", p=P))
-        targets = held.tile([D, M], BF16, name="targets")
-        nc.scalar.dma_start(targets[:], w)
 
         identity = held.tile([P, P], BF16, name="identity")
         make_identity(nc, identity[:])
         ones = held.tile([D, 1], F32, name="ones")
         nc.vector.memset(ones[:], 1.0)
-
-        row_squares = held.tile([P, S_BLOCKS, D], F32, name="row_squares")
-        nc.vector.tensor_tensor(row_squares[:], rows[:], rows[:], MULT)
-        row_sums = held.tile([P, S_BLOCKS], F32, name="row_sums")
-        nc.vector.tensor_reduce(row_sums[:], row_squares[:], mybir.AxisListType.X, ADD)
-        row_norms = held.tile([P, S_BLOCKS], F32, name="row_norms")
-        nc.scalar.activation(row_norms[:], row_sums[:], SQRT)
-        row_scales = held.tile([P, S_BLOCKS], F32, name="row_scales")
-        nc.vector.reciprocal(row_scales[:], row_norms[:])
-
-        unit_rows = held.tile([P, S_BLOCKS, D], BF16, name="unit_rows")
-        flipped = once.tile([D, S], BF16, name="flipped")
-        for b in range(S_BLOCKS):
-            nc.vector.tensor_scalar(
-                unit_rows[:, b, :], rows[:, b, :], row_scales[:, b : b + 1], None, op0=MULT
-            )
-            nc.tensor.transpose(flipped[:, b * P : (b + 1) * P], unit_rows[:, b, :], identity[:])
-        window = held.tile([D, S], BF16, name="window")
-        nc.vector.tensor_copy(window[:], flipped[:])
 
         target_squares = held.tile([D, M], F32, name="target_squares")
         nc.gpsimd.tensor_tensor(target_squares[:], targets[:], targets[:], MULT)
@@ -66,8 +53,47 @@ def tile_optimaltransportloss_kernel(tc, table, w, offs, out):
                 start=True,
                 stop=True,
             )
+
+        squares = [held.tile([P, D], F32, name=f"squares{h}") for h in range(HALVES)]
+        row_sums = [held.tile([P, HALF_BLOCKS], F32, name=f"row_sums{h}") for h in range(HALVES)]
+        for k in range(HALF_BLOCKS):
+            nc.scalar.activation(
+                squares[0][:], rows[0][:, k, :], SQUARE, accum_out=row_sums[0][:, k : k + 1]
+            )
+            nc.vector.scalar_tensor_tensor(
+                squares[1][:],
+                rows[1][:, k, :],
+                1.0,
+                rows[1][:, k, :],
+                op0=MULT,
+                op1=MULT,
+                accum_out=row_sums[1][:, k : k + 1],
+            )
+
+        row_norms = [held.tile([P, HALF_BLOCKS], F32, name=f"row_norms{h}") for h in range(HALVES)]
+        for h in range(HALVES):
+            nc.scalar.activation(row_norms[h][:], row_sums[h][:], SQRT)
         target_norms = held.tile([P, M_BLOCKS], F32, name="target_norms")
         nc.scalar.activation(target_norms[:], target_sums[:], SQRT)
+
+        window = held.tile([D, S], BF16, name="window")
+        for h in range(HALVES):
+            row_scales = held.tile([P, HALF_BLOCKS], F32, name=f"row_scales{h}")
+            nc.vector.reciprocal(row_scales[:], row_norms[h][:])
+            unit_rows = held.tile([P, HALF_BLOCKS, D], BF16, name=f"unit_rows{h}")
+            flipped = once.tile([D, HALF], BF16, name=f"flipped{h}")
+            for k in range(HALF_BLOCKS):
+                nc.vector.tensor_scalar(
+                    unit_rows[:, k, :], rows[h][:, k, :], row_scales[:, k : k + 1], None, op0=MULT
+                )
+                nc.tensor.transpose(
+                    flipped[:, k * P : (k + 1) * P], unit_rows[:, k, :], identity[:]
+                )
+            if h == 0:
+                nc.scalar.copy(window[:, :HALF], flipped[:])
+            else:
+                nc.vector.tensor_copy(window[:, HALF:], flipped[:])
+
         target_scales = held.tile([P, M_BLOCKS], F32, name="target_scales")
         nc.vector.reciprocal(target_scales[:], target_norms[:])
         minus_scales = held.tile([P, M_BLOCKS], F32, name="minus_scales")

@@ -9,8 +9,9 @@ COPY = mybir.ActivationFunctionType.Copy
 
 P = 128
 S, D, M, N = 1024, 128, 512, 1024
-HALVES = 2
-HALF = S // HALVES
+S_BLOCKS = S // P
+PAIRS = S_BLOCKS // 2
+HALF = S // 2
 HALF_BLOCKS = HALF // P
 M_BLOCKS = M // P
 PIECE = 512
@@ -28,10 +29,10 @@ def tile_optimaltransportloss_kernel(tc, table, w, offs, out):
         tc.psum_pool(name="once", bufs=1) as once,
         tc.psum_pool(name="banks", bufs=5) as banks,
     ):
-        table_halves = table.rearrange("(h k p) d -> h p k d", h=HALVES, p=P)
-        rows = [held.tile([P, HALF_BLOCKS, D], BF16, name=f"rows{h}") for h in range(HALVES)]
-        nc.scalar.dma_start(rows[0][:], table_halves[0])
-        nc.sync.dma_start(rows[1][:], table_halves[1])
+        table_pairs = table.rearrange("(q e p) d -> q p e d", q=PAIRS, p=P)
+        rows = [held.tile([P, 2, D], BF16, name=f"rows{q}") for q in range(PAIRS)]
+        for q in range(PAIRS):
+            nc.sync.dma_start(rows[q][:], table_pairs[q])
         targets = held.tile([D, M], BF16, name="targets")
         nc.sync.dma_start(targets[:], w)
         offsets = held.tile([P, N // 16], U16, name="offsets")
@@ -39,61 +40,65 @@ def tile_optimaltransportloss_kernel(tc, table, w, offs, out):
 
         identity = held.tile([P, P], BF16, name="identity")
         make_identity(nc, identity[:])
-        ones = held.tile([D, 1], F32, name="ones")
-        nc.vector.memset(ones[:], 1.0)
 
-        target_squares = held.tile([D, M], F32, name="target_squares")
-        nc.gpsimd.tensor_tensor(target_squares[:], targets[:], targets[:], MULT)
-        target_sums = once.tile([P, M_BLOCKS], F32, name="target_sums")
-        for mb in range(M_BLOCKS):
-            nc.tensor.matmul(
-                target_sums[:, mb : mb + 1],
-                target_squares[:, mb * P : (mb + 1) * P],
-                ones[:],
-                start=True,
-                stop=True,
-            )
+        unity = held.tile([P, 1], F32, name="unity")
+        nc.vector.memset(unity[:], 1.0)
+        nc.scalar.activation(unity[:], unity[:], SQRT)
 
-        squares = [held.tile([P, D], F32, name=f"squares{h}") for h in range(HALVES)]
-        row_sums = [held.tile([P, HALF_BLOCKS], F32, name=f"row_sums{h}") for h in range(HALVES)]
-        for k in range(HALF_BLOCKS):
+        squares = [held.tile([P, D], F32, name=f"squares{e}") for e in range(2)]
+        row_sums = [held.tile([P, PAIRS], F32, name=f"row_sums{e}") for e in range(2)]
+        for q in range(PAIRS):
             nc.scalar.activation(
-                squares[0][:], rows[0][:, k, :], SQUARE, accum_out=row_sums[0][:, k : k + 1]
+                squares[0][:], rows[q][:, 0, :], SQUARE, accum_out=row_sums[0][:, q : q + 1]
             )
             nc.vector.scalar_tensor_tensor(
                 squares[1][:],
-                rows[1][:, k, :],
+                rows[q][:, 1, :],
                 1.0,
-                rows[1][:, k, :],
+                rows[q][:, 1, :],
                 op0=MULT,
                 op1=MULT,
-                accum_out=row_sums[1][:, k : k + 1],
+                accum_out=row_sums[1][:, q : q + 1],
             )
 
-        row_norms = [held.tile([P, HALF_BLOCKS], F32, name=f"row_norms{h}") for h in range(HALVES)]
-        for h in range(HALVES):
-            nc.scalar.activation(row_norms[h][:], row_sums[h][:], SQRT)
+        row_norms = [held.tile([P, PAIRS], F32, name=f"row_norms{e}") for e in range(2)]
+        row_scales = [held.tile([P, PAIRS], F32, name=f"row_scales{e}") for e in range(2)]
+        for e in range(2):
+            nc.scalar.activation(row_norms[e][:], row_sums[e][:], SQRT)
+            nc.vector.reciprocal(row_scales[e][:], row_norms[e][:])
+
+        gram = once.tile([P, M_BLOCKS, P], F32, name="gram")
+        for mb in range(M_BLOCKS):
+            block = targets[:, mb * P : (mb + 1) * P]
+            nc.tensor.matmul(gram[:, mb, :], block, block, start=True, stop=True)
+
+        unit_rows = held.tile([P, S_BLOCKS, D], BF16, name="unit_rows")
+        flipped = [once.tile([D, HALF], BF16, name=f"flipped{h}") for h in range(2)]
+        window = held.tile([D, S], BF16, name="window")
+        for b in range(S_BLOCKS):
+            q, e = divmod(b, 2)
+            h, k = divmod(b, HALF_BLOCKS)
+            nc.vector.tensor_scalar(
+                unit_rows[:, b, :], rows[q][:, e, :], row_scales[e][:, q : q + 1], None, op0=MULT
+            )
+            nc.tensor.transpose(flipped[h][:, k * P : (k + 1) * P], unit_rows[:, b, :], identity[:])
+        nc.scalar.copy(window[:, :HALF], flipped[0][:])
+        nc.vector.tensor_copy(window[:, HALF:], flipped[1][:])
+
+        diagonal = held.tile([P, P], F32, name="diagonal")
+        target_sums = held.tile([P, M_BLOCKS], F32, name="target_sums")
+        for mb in range(M_BLOCKS):
+            nc.vector.scalar_tensor_tensor(
+                diagonal[:],
+                gram[:, mb, :],
+                1.0,
+                identity[:],
+                op0=MULT,
+                op1=MULT,
+                accum_out=target_sums[:, mb : mb + 1],
+            )
         target_norms = held.tile([P, M_BLOCKS], F32, name="target_norms")
         nc.scalar.activation(target_norms[:], target_sums[:], SQRT)
-
-        window = held.tile([D, S], BF16, name="window")
-        for h in range(HALVES):
-            row_scales = held.tile([P, HALF_BLOCKS], F32, name=f"row_scales{h}")
-            nc.vector.reciprocal(row_scales[:], row_norms[h][:])
-            unit_rows = held.tile([P, HALF_BLOCKS, D], BF16, name=f"unit_rows{h}")
-            flipped = once.tile([D, HALF], BF16, name=f"flipped{h}")
-            for k in range(HALF_BLOCKS):
-                nc.vector.tensor_scalar(
-                    unit_rows[:, k, :], rows[h][:, k, :], row_scales[:, k : k + 1], None, op0=MULT
-                )
-                nc.tensor.transpose(
-                    flipped[:, k * P : (k + 1) * P], unit_rows[:, k, :], identity[:]
-                )
-            if h == 0:
-                nc.scalar.copy(window[:, :HALF], flipped[:])
-            else:
-                nc.vector.tensor_copy(window[:, HALF:], flipped[:])
-
         target_scales = held.tile([P, M_BLOCKS], F32, name="target_scales")
         nc.vector.reciprocal(target_scales[:], target_norms[:])
         minus_scales = held.tile([P, M_BLOCKS], F32, name="minus_scales")

@@ -18,6 +18,9 @@ PIECE = 512
 PIECES = N // PIECE
 PIECE_COLUMNS = PIECE // 16
 
+WARM_BEFORE = 6
+WARM_AFTER = 2
+
 FLOPS = 2 * M * N * D
 
 
@@ -27,7 +30,7 @@ def tile_optimaltransportloss_kernel(tc, table, w, offs, out):
         tc.tile_pool(name="held", bufs=1) as held,
         tc.tile_pool(name="staged", bufs=M_BLOCKS * PIECES) as staged,
         tc.psum_pool(name="once", bufs=1) as once,
-        tc.psum_pool(name="banks", bufs=5) as banks,
+        tc.psum_pool(name="banks", bufs=4) as banks,
     ):
         table_pairs = table.rearrange("(q e p) d -> q p e d", q=PAIRS, p=P)
         rows = [held.tile([P, 2, D], BF16, name=f"rows{q}") for q in range(PAIRS)]
@@ -44,6 +47,12 @@ def tile_optimaltransportloss_kernel(tc, table, w, offs, out):
         unity = held.tile([P, 1], F32, name="unity")
         nc.vector.memset(unity[:], 1.0)
         nc.scalar.activation(unity[:], unity[:], SQRT)
+
+        zeros = held.tile([P, PIECE], BF16, name="zeros")
+        nc.vector.memset(zeros[:], 0.0)
+        unread = once.tile([P, PIECE], F32, name="unread")
+        for turn in range(WARM_BEFORE):
+            nc.tensor.matmul(unread[:], zeros[:, :P], zeros[:], start=True, stop=True)
 
         squares = [held.tile([P, D], F32, name=f"squares{e}") for e in range(2)]
         row_sums = [held.tile([P, PAIRS], F32, name=f"row_sums{e}") for e in range(2)]
@@ -82,6 +91,8 @@ def tile_optimaltransportloss_kernel(tc, table, w, offs, out):
                 unit_rows[:, b, :], rows[q][:, e, :], row_scales[e][:, q : q + 1], None, op0=MULT
             )
             nc.tensor.transpose(flipped[h][:, k * P : (k + 1) * P], unit_rows[:, b, :], identity[:])
+        for turn in range(WARM_AFTER):
+            nc.tensor.matmul(unread[:], zeros[:, :P], zeros[:], start=True, stop=True)
         nc.scalar.copy(window[:, :HALF], flipped[0][:])
         nc.vector.tensor_copy(window[:, HALF:], flipped[1][:])
 

@@ -3,22 +3,21 @@ from concourse.masks import make_identity
 
 BF16, F32, U16 = mybir.dt.bfloat16, mybir.dt.float32, mybir.dt.uint16
 MULT, ADD = mybir.AluOpType.mult, mybir.AluOpType.add
-SQRT = mybir.ActivationFunctionType.Sqrt
+RSQRT = mybir.ActivationFunctionType.Abs_reciprocal_sqrt
 SQUARE = mybir.ActivationFunctionType.Square
 COPY = mybir.ActivationFunctionType.Copy
 
 P = 128
 S, D, M, N = 1024, 128, 512, 1024
-S_BLOCKS = S // P
-PAIRS = S_BLOCKS // 2
-HALF = S // 2
-HALF_BLOCKS = HALF // P
+QUARTERS = 4
+QUARTER = S // QUARTERS
 M_BLOCKS = M // P
 PIECE = 512
 PIECES = N // PIECE
 PIECE_COLUMNS = PIECE // 16
+APART = 8
 
-WARM_BEFORE = 6
+WARM_BEFORE = 4
 WARM_AFTER = 2
 
 FLOPS = 2 * M * N * D
@@ -28,25 +27,26 @@ def tile_optimaltransportloss_kernel(tc, table, w, offs, out):
     nc = tc.nc
     with (
         tc.tile_pool(name="held", bufs=1) as held,
+        tc.tile_pool(name="parts", bufs=QUARTERS) as parts,
         tc.tile_pool(name="staged", bufs=M_BLOCKS * PIECES) as staged,
         tc.psum_pool(name="once", bufs=1) as once,
-        tc.psum_pool(name="banks", bufs=4) as banks,
+        tc.psum_pool(name="banks", bufs=6) as banks,
     ):
-        table_pairs = table.rearrange("(q e p) d -> q p e d", q=PAIRS, p=P)
-        rows = [held.tile([P, 2, D], BF16, name=f"rows{q}") for q in range(PAIRS)]
-        for q in range(PAIRS):
-            nc.sync.dma_start(rows[q][:], table_pairs[q])
+        table_parts = table.rearrange("(q e p) d -> q p e d", q=QUARTERS, p=P)
+        rows = [parts.tile([P, 2, D], BF16, name="rows") for q in range(QUARTERS)]
+        for q in range(QUARTERS):
+            nc.sync.dma_start(rows[q][:], table_parts[q])
         targets = held.tile([D, M], BF16, name="targets")
         nc.sync.dma_start(targets[:], w)
         offsets = held.tile([P, N // 16], U16, name="offsets")
         nc.sync.dma_start(offsets[:], offs)
 
+        unity = held.tile([P, 1], F32, name="unity")
+        nc.gpsimd.memset(unity[:], 1.0)
+        nc.scalar.activation(unity[:], unity[:], RSQRT)
+
         identity = held.tile([P, P], BF16, name="identity")
         make_identity(nc, identity[:])
-
-        unity = held.tile([P, 1], F32, name="unity")
-        nc.vector.memset(unity[:], 1.0)
-        nc.scalar.activation(unity[:], unity[:], SQRT)
 
         zeros = held.tile([P, PIECE], BF16, name="zeros")
         nc.vector.memset(zeros[:], 0.0)
@@ -54,73 +54,75 @@ def tile_optimaltransportloss_kernel(tc, table, w, offs, out):
         for turn in range(WARM_BEFORE):
             nc.tensor.matmul(unread[:], zeros[:, :P], zeros[:], start=True, stop=True)
 
-        squares = [held.tile([P, D], F32, name=f"squares{e}") for e in range(2)]
-        row_sums = [held.tile([P, PAIRS], F32, name=f"row_sums{e}") for e in range(2)]
-        for q in range(PAIRS):
+        flipped_targets = once.tile([P, M_BLOCKS, D], BF16, name="flipped_targets")
+        for mb in range(M_BLOCKS):
+            nc.tensor.transpose(
+                flipped_targets[:, mb, :], targets[:, mb * P : (mb + 1) * P], identity[:]
+            )
+
+        window = held.tile([D, S], BF16, name="window")
+        scalar_squares = held.tile([P, D], F32, name="scalar_squares")
+        vector_squares = held.tile([P, D], F32, name="vector_squares")
+        scales = [parts.tile([P, 2], F32, name="scales") for q in range(QUARTERS)]
+        flipped = [
+            banks.tile([D, QUARTER], BF16, name="flipped", tag="bank") for q in range(QUARTERS)
+        ]
+
+        def measure(q):
+            sums = parts.tile([P, 2, APART], F32, name="sums")
             nc.scalar.activation(
-                squares[0][:], rows[q][:, 0, :], SQUARE, accum_out=row_sums[0][:, q : q + 1]
+                scalar_squares[:], rows[q][:, 0, :], SQUARE, accum_out=sums[:, 0, 0:1]
             )
             nc.vector.scalar_tensor_tensor(
-                squares[1][:],
+                vector_squares[:],
                 rows[q][:, 1, :],
                 1.0,
                 rows[q][:, 1, :],
                 op0=MULT,
                 op1=MULT,
-                accum_out=row_sums[1][:, q : q + 1],
+                accum_out=sums[:, 1, 0:1],
             )
+            nc.scalar.activation(scales[q][:], sums[:, :, 0], RSQRT)
 
-        row_norms = [held.tile([P, PAIRS], F32, name=f"row_norms{e}") for e in range(2)]
-        row_scales = [held.tile([P, PAIRS], F32, name=f"row_scales{e}") for e in range(2)]
-        for e in range(2):
-            nc.scalar.activation(row_norms[e][:], row_sums[e][:], SQRT)
-            nc.vector.reciprocal(row_scales[e][:], row_norms[e][:])
+        def normalise(q):
+            unit_rows = parts.tile([P, 2, D], BF16, name="unit_rows")
+            for e in range(2):
+                nc.vector.tensor_scalar(
+                    unit_rows[:, e, :], rows[q][:, e, :], scales[q][:, e : e + 1], None, op0=MULT
+                )
+                nc.tensor.transpose(
+                    flipped[q][:, e * P : (e + 1) * P], unit_rows[:, e, :], identity[:]
+                )
 
-        gram = once.tile([P, M_BLOCKS, P], F32, name="gram")
-        for mb in range(M_BLOCKS):
-            block = targets[:, mb * P : (mb + 1) * P]
-            nc.tensor.matmul(gram[:, mb, :], block, block, start=True, stop=True)
-
-        unit_rows = held.tile([P, S_BLOCKS, D], BF16, name="unit_rows")
-        flipped = [once.tile([D, HALF], BF16, name=f"flipped{h}") for h in range(2)]
-        window = held.tile([D, S], BF16, name="window")
-        for b in range(S_BLOCKS):
-            q, e = divmod(b, 2)
-            h, k = divmod(b, HALF_BLOCKS)
-            nc.vector.tensor_scalar(
-                unit_rows[:, b, :], rows[q][:, e, :], row_scales[e][:, q : q + 1], None, op0=MULT
-            )
-            nc.tensor.transpose(flipped[h][:, k * P : (k + 1) * P], unit_rows[:, b, :], identity[:])
+        measure(0)
+        for q in range(1, QUARTERS):
+            measure(q)
+            normalise(q - 1)
+        normalise(QUARTERS - 1)
+        for q in range(QUARTERS):
+            nc.vector.tensor_copy(window[:, q * QUARTER : (q + 1) * QUARTER], flipped[q][:])
         for turn in range(WARM_AFTER):
             nc.tensor.matmul(unread[:], zeros[:, :P], zeros[:], start=True, stop=True)
-        nc.scalar.copy(window[:, :HALF], flipped[0][:])
-        nc.vector.tensor_copy(window[:, HALF:], flipped[1][:])
 
-        diagonal = held.tile([P, P], F32, name="diagonal")
         target_sums = held.tile([P, M_BLOCKS], F32, name="target_sums")
         for mb in range(M_BLOCKS):
-            nc.vector.scalar_tensor_tensor(
-                diagonal[:],
-                gram[:, mb, :],
-                1.0,
-                identity[:],
-                op0=MULT,
-                op1=MULT,
+            nc.scalar.activation(
+                scalar_squares[:],
+                flipped_targets[:, mb, :],
+                SQUARE,
                 accum_out=target_sums[:, mb : mb + 1],
             )
-        target_norms = held.tile([P, M_BLOCKS], F32, name="target_norms")
-        nc.scalar.activation(target_norms[:], target_sums[:], SQRT)
         target_scales = held.tile([P, M_BLOCKS], F32, name="target_scales")
-        nc.vector.reciprocal(target_scales[:], target_norms[:])
+        nc.scalar.activation(target_scales[:], target_sums[:], RSQRT)
         minus_scales = held.tile([P, M_BLOCKS], F32, name="minus_scales")
-        nc.vector.tensor_scalar(minus_scales[:], target_scales[:], -1.0, None, op0=MULT)
+        nc.scalar.mul(minus_scales[:], target_scales[:], -1.0)
 
         for mb in range(M_BLOCKS):
             for piece in range(PIECES):
                 looked_up = window[:].indirect(
                     offsets[:, piece * PIECE_COLUMNS : (piece + 1) * PIECE_COLUMNS]
                 )
-                product = banks.tile([P, PIECE], F32, name="product")
+                product = banks.tile([P, PIECE], F32, name="product", tag="bank")
                 nc.tensor.matmul(
                     product[:], targets[:, mb * P : (mb + 1) * P], looked_up, start=True, stop=True
                 )

@@ -12,7 +12,8 @@ S, D, M, N = 1024, 128, 512, 1024
 QUARTERS = 4
 QUARTER = S // QUARTERS
 M_BLOCKS = M // P
-PIECE = 512
+BANK = 512
+PIECE = 256
 PIECES = N // PIECE
 PIECE_COLUMNS = PIECE // 16
 APART = 8
@@ -48,9 +49,9 @@ def tile_optimaltransportloss_kernel(tc, table, w, offs, out):
         identity = held.tile([P, P], BF16, name="identity")
         make_identity(nc, identity[:])
 
-        zeros = held.tile([P, PIECE], BF16, name="zeros")
+        zeros = held.tile([P, BANK], BF16, name="zeros")
         nc.vector.memset(zeros[:], 0.0)
-        unread = once.tile([P, PIECE], F32, name="unread")
+        unread = once.tile([P, BANK], F32, name="unread")
         for turn in range(WARM_BEFORE):
             nc.tensor.matmul(unread[:], zeros[:, :P], zeros[:], start=True, stop=True)
 
@@ -63,15 +64,10 @@ def tile_optimaltransportloss_kernel(tc, table, w, offs, out):
         window = held.tile([D, S], BF16, name="window")
         scalar_squares = held.tile([P, D], F32, name="scalar_squares")
         vector_squares = held.tile([P, D], F32, name="vector_squares")
-        scales = [parts.tile([P, 2], F32, name="scales") for q in range(QUARTERS)]
-        flipped = [
-            banks.tile([D, QUARTER], BF16, name="flipped", tag="bank") for q in range(QUARTERS)
-        ]
-
-        def measure(q):
-            sums = parts.tile([P, 2, APART], F32, name="sums")
+        sums = [parts.tile([P, 2, APART], F32, name="sums") for q in range(QUARTERS)]
+        for q in range(QUARTERS):
             nc.scalar.activation(
-                scalar_squares[:], rows[q][:, 0, :], SQUARE, accum_out=sums[:, 0, 0:1]
+                scalar_squares[:], rows[q][:, 0, :], SQUARE, accum_out=sums[q][:, 0, 0:1]
             )
             nc.vector.scalar_tensor_tensor(
                 vector_squares[:],
@@ -80,11 +76,15 @@ def tile_optimaltransportloss_kernel(tc, table, w, offs, out):
                 rows[q][:, 1, :],
                 op0=MULT,
                 op1=MULT,
-                accum_out=sums[:, 1, 0:1],
+                accum_out=sums[q][:, 1, 0:1],
             )
-            nc.scalar.activation(scales[q][:], sums[:, :, 0], RSQRT)
-
-        def normalise(q):
+        scales = [parts.tile([P, 2], F32, name="scales") for q in range(QUARTERS)]
+        for q in range(QUARTERS):
+            nc.scalar.activation(scales[q][:], sums[q][:, :, 0], RSQRT)
+        flipped = [
+            banks.tile([D, QUARTER], BF16, name="flipped", tag="bank") for q in range(QUARTERS)
+        ]
+        for q in range(QUARTERS):
             unit_rows = parts.tile([P, 2, D], BF16, name="unit_rows")
             for e in range(2):
                 nc.vector.tensor_scalar(
@@ -93,12 +93,6 @@ def tile_optimaltransportloss_kernel(tc, table, w, offs, out):
                 nc.tensor.transpose(
                     flipped[q][:, e * P : (e + 1) * P], unit_rows[:, e, :], identity[:]
                 )
-
-        measure(0)
-        for q in range(1, QUARTERS):
-            measure(q)
-            normalise(q - 1)
-        normalise(QUARTERS - 1)
         for q in range(QUARTERS):
             nc.vector.tensor_copy(window[:, q * QUARTER : (q + 1) * QUARTER], flipped[q][:])
         for turn in range(WARM_AFTER):

@@ -29,7 +29,7 @@ def tile_optimaltransportloss_kernel(tc, table, w, offs, out):
     with (
         tc.tile_pool(name="held", bufs=1) as held,
         tc.tile_pool(name="parts", bufs=QUARTERS) as parts,
-        tc.tile_pool(name="staged", bufs=M_BLOCKS * PIECES) as staged,
+        tc.tile_pool(name="staged", bufs=M_BLOCKS * PIECES + 2) as staged,
         tc.psum_pool(name="once", bufs=1) as once,
         tc.psum_pool(name="banks", bufs=6) as banks,
     ):
@@ -112,6 +112,7 @@ def tile_optimaltransportloss_kernel(tc, table, w, offs, out):
         nc.scalar.mul(minus_scales[:], target_scales[:], -1.0)
 
         for mb in range(M_BLOCKS):
+            minus_scale = minus_scales[:, mb : mb + 1]
             for piece in range(PIECES):
                 looked_up = window[:].indirect(
                     offsets[:, piece * PIECE_COLUMNS : (piece + 1) * PIECE_COLUMNS]
@@ -120,14 +121,31 @@ def tile_optimaltransportloss_kernel(tc, table, w, offs, out):
                 nc.tensor.matmul(
                     product[:], targets[:, mb * P : (mb + 1) * P], looked_up, start=True, stop=True
                 )
-                distance = staged.tile([P, PIECE], F32, name="distance")
-                minus_scale = minus_scales[:, mb : mb + 1]
-                if piece % 2 == 0:
-                    nc.vector.tensor_scalar(
-                        distance[:], product[:], minus_scale, 1.0, op0=MULT, op1=ADD
+                outermost = (mb, piece) in ((0, 0), (M_BLOCKS - 1, PIECES - 1))
+                columns = PIECE // 2 if outermost else PIECE
+                for begin in range(0, PIECE, columns):
+                    distance = staged.tile([P, columns], F32, name="distance")
+                    if piece % 2 == 0:
+                        nc.vector.tensor_scalar(
+                            distance[:],
+                            product[:, begin : begin + columns],
+                            minus_scale,
+                            1.0,
+                            op0=MULT,
+                            op1=ADD,
+                        )
+                    else:
+                        nc.scalar.activation(
+                            distance[:],
+                            product[:, begin : begin + columns],
+                            COPY,
+                            bias=1.0,
+                            scale=minus_scale,
+                        )
+                    nc.sync.dma_start(
+                        out[
+                            mb * P : (mb + 1) * P,
+                            piece * PIECE + begin : piece * PIECE + begin + columns,
+                        ],
+                        distance[:],
                     )
-                else:
-                    nc.scalar.activation(distance[:], product[:], COPY, bias=1.0, scale=minus_scale)
-                nc.sync.dma_start(
-                    out[mb * P : (mb + 1) * P, piece * PIECE : (piece + 1) * PIECE], distance[:]
-                )

@@ -62,10 +62,10 @@ def tile_optimaltransportloss_kernel(tc, table, w, offs, out):
             )
 
         window = held.tile([D, S], BF16, name="window")
-        scalar_squares = held.tile([P, D], F32, name="scalar_squares")
-        vector_squares = held.tile([P, D], F32, name="vector_squares")
         sums = [parts.tile([P, 2, APART], F32, name="sums") for q in range(QUARTERS)]
         for q in range(QUARTERS):
+            scalar_squares = parts.tile([P, D], F32, name="scalar_squares")
+            vector_squares = parts.tile([P, D], F32, name="vector_squares")
             nc.scalar.activation(
                 scalar_squares[:], rows[q][:, 0, :], SQUARE, accum_out=sums[q][:, 0, 0:1]
             )
@@ -100,8 +100,9 @@ def tile_optimaltransportloss_kernel(tc, table, w, offs, out):
 
         target_sums = held.tile([P, M_BLOCKS], F32, name="target_sums")
         for mb in range(M_BLOCKS):
+            target_squares = parts.tile([P, D], F32, name="target_squares")
             nc.scalar.activation(
-                scalar_squares[:],
+                target_squares[:],
                 flipped_targets[:, mb, :],
                 SQUARE,
                 accum_out=target_sums[:, mb : mb + 1],

@@ -10,6 +10,7 @@ COPY = mybir.ActivationFunctionType.Copy
 P = 128
 S, D, M, N = 1024, 128, 512, 1024
 QUARTERS = 4
+PAIRED = QUARTERS // 2
 QUARTER = S // QUARTERS
 M_BLOCKS = M // P
 BANK = 512
@@ -33,10 +34,11 @@ def tile_optimaltransportloss_kernel(tc, table, w, offs, out):
         tc.psum_pool(name="once", bufs=1) as once,
         tc.psum_pool(name="banks", bufs=6) as banks,
     ):
-        table_parts = table.rearrange("(q e p) d -> q p e d", q=QUARTERS, p=P)
+        by_pairs = table.rearrange("(q p e) d -> q p e d", q=QUARTERS, p=P)
+        by_blocks = table.rearrange("(q e p) d -> q p e d", q=QUARTERS, p=P)
         rows = [parts.tile([P, 2, D], BF16, name="rows") for q in range(QUARTERS)]
         for q in range(QUARTERS):
-            nc.sync.dma_start(rows[q][:], table_parts[q])
+            nc.sync.dma_start(rows[q][:], by_pairs[q] if q < PAIRED else by_blocks[q])
         targets = held.tile([D, M], BF16, name="targets")
         nc.sync.dma_start(targets[:], w)
         offsets = held.tile([P, N // 16], U16, name="offsets")
@@ -82,7 +84,7 @@ def tile_optimaltransportloss_kernel(tc, table, w, offs, out):
         for q in range(QUARTERS):
             nc.scalar.activation(scales[q][:], sums[q][:, :, 0], RSQRT)
         flipped = [
-            banks.tile([D, QUARTER], BF16, name="flipped", tag="bank") for q in range(QUARTERS)
+            banks.tile([D, 2, P], BF16, name="flipped", tag="bank") for q in range(QUARTERS)
         ]
         for q in range(QUARTERS):
             unit_rows = parts.tile([P, 2, D], BF16, name="unit_rows")
@@ -90,11 +92,16 @@ def tile_optimaltransportloss_kernel(tc, table, w, offs, out):
                 nc.vector.tensor_scalar(
                     unit_rows[:, e, :], rows[q][:, e, :], scales[q][:, e : e + 1], None, op0=MULT
                 )
-                nc.tensor.transpose(
-                    flipped[q][:, e * P : (e + 1) * P], unit_rows[:, e, :], identity[:]
-                )
+                nc.tensor.transpose(flipped[q][:, e, :], unit_rows[:, e, :], identity[:])
         for q in range(QUARTERS):
-            nc.vector.tensor_copy(window[:, q * QUARTER : (q + 1) * QUARTER], flipped[q][:])
+            columns = window[:, q * QUARTER : (q + 1) * QUARTER]
+            if q < PAIRED:
+                nc.vector.tensor_copy(
+                    columns.rearrange("d (p e) -> d p e", e=2),
+                    flipped[q][:].rearrange("d e p -> d p e"),
+                )
+            else:
+                nc.vector.tensor_copy(columns, flipped[q][:].rearrange("d e p -> d (e p)"))
         for turn in range(WARM_AFTER):
             nc.tensor.matmul(unread[:], zeros[:, :P], zeros[:], start=True, stop=True)
 

@@ -17,10 +17,8 @@ BANK = 512
 PIECE = 256
 PIECES = N // PIECE
 PIECE_COLUMNS = PIECE // 16
-APART = 8
 
 WARM_BEFORE = 4
-WARM_AFTER = 2
 
 FLOPS = 2 * M * N * D
 
@@ -30,6 +28,7 @@ def tile_optimaltransportloss_kernel(tc, table, w, offs, out):
     with (
         tc.tile_pool(name="held", bufs=1) as held,
         tc.tile_pool(name="parts", bufs=QUARTERS) as parts,
+        tc.tile_pool(name="unread_squares", bufs=2 * QUARTERS) as unread_squares,
         tc.tile_pool(name="staged", bufs=M_BLOCKS * PIECES + 2) as staged,
         tc.psum_pool(name="once", bufs=1) as once,
         tc.psum_pool(name="banks", bufs=6) as banks,
@@ -64,25 +63,20 @@ def tile_optimaltransportloss_kernel(tc, table, w, offs, out):
             )
 
         window = held.tile([D, S], BF16, name="window")
-        sums = [parts.tile([P, 2, APART], F32, name="sums") for q in range(QUARTERS)]
+        sums = [parts.tile([P, 2], F32, name="sums") for q in range(QUARTERS)]
         for q in range(QUARTERS):
-            scalar_squares = parts.tile([P, D], F32, name="scalar_squares")
-            vector_squares = parts.tile([P, D], F32, name="vector_squares")
-            nc.scalar.activation(
-                scalar_squares[:], rows[q][:, 0, :], SQUARE, accum_out=sums[q][:, 0, 0:1]
-            )
-            nc.vector.scalar_tensor_tensor(
-                vector_squares[:],
-                rows[q][:, 1, :],
-                1.0,
-                rows[q][:, 1, :],
-                op0=MULT,
-                op1=MULT,
-                accum_out=sums[q][:, 1, 0:1],
-            )
+            for e in range(2):
+                squares = unread_squares.tile([P, D], F32, name="squares")
+                block, total = rows[q][:, e, :], sums[q][:, e : e + 1]
+                if q % 2 == 0:
+                    nc.scalar.activation(squares[:], block, SQUARE, accum_out=total)
+                else:
+                    nc.vector.scalar_tensor_tensor(
+                        squares[:], block, 1.0, block, op0=MULT, op1=MULT, accum_out=total
+                    )
         scales = [parts.tile([P, 2], F32, name="scales") for q in range(QUARTERS)]
         for q in range(QUARTERS):
-            nc.scalar.activation(scales[q][:], sums[q][:, :, 0], RSQRT)
+            nc.scalar.activation(scales[q][:], sums[q][:], RSQRT)
         flipped = [
             banks.tile([D, 2, P], BF16, name="flipped", tag="bank") for q in range(QUARTERS)
         ]
@@ -102,8 +96,6 @@ def tile_optimaltransportloss_kernel(tc, table, w, offs, out):
                 )
             else:
                 nc.vector.tensor_copy(columns, flipped[q][:].rearrange("d e p -> d (e p)"))
-        for turn in range(WARM_AFTER):
-            nc.tensor.matmul(unread[:], zeros[:, :P], zeros[:], start=True, stop=True)
 
         target_sums = held.tile([P, M_BLOCKS], F32, name="target_sums")
         for mb in range(M_BLOCKS):

@@ -29,6 +29,7 @@ def tile_optimaltransportloss_kernel(tc, table, w, offs, out):
         tc.tile_pool(name="held", bufs=1) as held,
         tc.tile_pool(name="parts", bufs=QUARTERS) as parts,
         tc.tile_pool(name="unread_squares", bufs=2 * QUARTERS) as unread_squares,
+        tc.tile_pool(name="sums_and_scales", bufs=2 * QUARTERS) as sums_and_scales,
         tc.tile_pool(name="staged", bufs=M_BLOCKS * PIECES + 2) as staged,
         tc.psum_pool(name="once", bufs=1) as once,
         tc.psum_pool(name="banks", bufs=6) as banks,
@@ -63,20 +64,20 @@ def tile_optimaltransportloss_kernel(tc, table, w, offs, out):
             )
 
         window = held.tile([D, S], BF16, name="window")
-        sums = [parts.tile([P, 2], F32, name="sums") for q in range(QUARTERS)]
+        sums = [sums_and_scales.tile([P, 1], F32, name="sums") for b in range(2 * QUARTERS)]
         for q in range(QUARTERS):
             for e in range(2):
                 squares = unread_squares.tile([P, D], F32, name="squares")
-                block, total = rows[q][:, e, :], sums[q][:, e : e + 1]
+                block, total = rows[q][:, e, :], sums[2 * q + e][:]
                 if q % 2 == 0:
                     nc.scalar.activation(squares[:], block, SQUARE, accum_out=total)
                 else:
                     nc.vector.scalar_tensor_tensor(
                         squares[:], block, 1.0, block, op0=MULT, op1=MULT, accum_out=total
                     )
-        scales = [parts.tile([P, 2], F32, name="scales") for q in range(QUARTERS)]
-        for q in range(QUARTERS):
-            nc.scalar.activation(scales[q][:], sums[q][:], RSQRT)
+        scales = [sums_and_scales.tile([P, 1], F32, name="scales") for b in range(2 * QUARTERS)]
+        for b in range(2 * QUARTERS):
+            nc.scalar.activation(scales[b][:], sums[b][:], RSQRT)
         flipped = [
             banks.tile([D, 2, P], BF16, name="flipped", tag="bank") for q in range(QUARTERS)
         ]
@@ -84,7 +85,7 @@ def tile_optimaltransportloss_kernel(tc, table, w, offs, out):
             unit_rows = parts.tile([P, 2, D], BF16, name="unit_rows")
             for e in range(2):
                 nc.vector.tensor_scalar(
-                    unit_rows[:, e, :], rows[q][:, e, :], scales[q][:, e : e + 1], None, op0=MULT
+                    unit_rows[:, e, :], rows[q][:, e, :], scales[2 * q + e][:], None, op0=MULT
                 )
                 nc.tensor.transpose(flipped[q][:, e, :], unit_rows[:, e, :], identity[:])
         for q in range(QUARTERS):

@@ -125,7 +125,7 @@ def tile_optimaltransportloss_kernel(tc, table, w, offs, out):
                 outermost = (mb, piece) in ((0, 0), (M_BLOCKS - 1, PIECES - 1))
                 columns = PIECE // 2 if outermost else PIECE
                 for begin in range(0, PIECE, columns):
-                    distance = staged.tile([P, columns], F32, name="distance")
+                    distance = staged.tile([P, columns], F32, name="distance", align_bytes=4 * PIECE)
                     if piece % 2 == 0:
                         nc.vector.tensor_scalar(
                             distance[:],

@@ -20,6 +20,8 @@ PIECE_COLUMNS = PIECE // 16
 
 WARM_BEFORE = 4
 
+ALIGNED = 1024
+
 FLOPS = 2 * M * N * D
 
 
@@ -36,12 +38,14 @@ def tile_optimaltransportloss_kernel(tc, table, w, offs, out):
     ):
         by_pairs = table.rearrange("(q p e) d -> q p e d", q=QUARTERS, p=P)
         by_blocks = table.rearrange("(q e p) d -> q p e d", q=QUARTERS, p=P)
-        rows = [parts.tile([P, 2, D], BF16, name="rows") for q in range(QUARTERS)]
+        rows = [
+            parts.tile([P, 2, D], BF16, name="rows", align_bytes=ALIGNED) for q in range(QUARTERS)
+        ]
         for q in range(QUARTERS):
             nc.sync.dma_start(rows[q][:], by_pairs[q] if q < PAIRED else by_blocks[q])
-        targets = held.tile([D, M], BF16, name="targets")
+        targets = held.tile([D, M], BF16, name="targets", align_bytes=ALIGNED)
         nc.sync.dma_start(targets[:], w)
-        offsets = held.tile([P, N // 16], U16, name="offsets")
+        offsets = held.tile([P, N // 16], U16, name="offsets", align_bytes=ALIGNED)
         nc.sync.dma_start(offsets[:], offs)
 
         unity = held.tile([P, 1], F32, name="unity")
@@ -69,7 +73,7 @@ def tile_optimaltransportloss_kernel(tc, table, w, offs, out):
             for e in range(2):
                 squares = unread_squares.tile([P, D], F32, name="squares")
                 block, total = rows[q][:, e, :], sums[2 * q + e][:]
-                if q % 2 == 0:
+                if (q, e) in ((0, 0), (0, 1), (2, 0), (3, 0)):
                     nc.scalar.activation(squares[:], block, SQUARE, accum_out=total)
                 else:
                     nc.vector.scalar_tensor_tensor(
@@ -125,7 +129,7 @@ def tile_optimaltransportloss_kernel(tc, table, w, offs, out):
                 outermost = (mb, piece) in ((0, 0), (M_BLOCKS - 1, PIECES - 1))
                 columns = PIECE // 2 if outermost else PIECE
                 for begin in range(0, PIECE, columns):
-                    distance = staged.tile([P, columns], F32, name="distance", align_bytes=4 * PIECE)
+                    distance = staged.tile([P, columns], F32, name="distance", align_bytes=ALIGNED)
                     if piece % 2 == 0:
                         nc.vector.tensor_scalar(
                             distance[:],

@@ -9,9 +9,9 @@ COPY = mybir.ActivationFunctionType.Copy
 
 P = 128
 S, D, M, N = 1024, 128, 512, 1024
-QUARTERS = 4
-PAIRED = QUARTERS // 2
-QUARTER = S // QUARTERS
+BLOCKS = S // P
+HALF, QUARTER = S // 2, S // 4
+HALF_BLOCKS = HALF // P
 M_BLOCKS = M // P
 BANK = 512
 PIECE = 256
@@ -29,20 +29,23 @@ def tile_optimaltransportloss_kernel(tc, table, w, offs, out):
     nc = tc.nc
     with (
         tc.tile_pool(name="held", bufs=1) as held,
-        tc.tile_pool(name="parts", bufs=QUARTERS) as parts,
-        tc.tile_pool(name="unread_squares", bufs=2 * QUARTERS) as unread_squares,
-        tc.tile_pool(name="sums_and_scales", bufs=2 * QUARTERS) as sums_and_scales,
+        tc.tile_pool(name="parts", bufs=M_BLOCKS) as parts,
+        tc.tile_pool(name="unread_squares", bufs=BLOCKS) as unread_squares,
+        tc.tile_pool(name="sums_and_scales", bufs=BLOCKS) as sums_and_scales,
+        tc.tile_pool(name="unit", bufs=BLOCKS) as unit,
         tc.tile_pool(name="staged", bufs=M_BLOCKS * PIECES + 2) as staged,
         tc.psum_pool(name="once", bufs=1) as once,
         tc.psum_pool(name="banks", bufs=6) as banks,
     ):
-        by_pairs = table.rearrange("(q p e) d -> q p e d", q=QUARTERS, p=P)
-        by_blocks = table.rearrange("(q e p) d -> q p e d", q=QUARTERS, p=P)
-        rows = [
-            parts.tile([P, 2, D], BF16, name="rows", align_bytes=ALIGNED) for q in range(QUARTERS)
-        ]
-        for q in range(QUARTERS):
-            nc.sync.dma_start(rows[q][:], by_pairs[q] if q < PAIRED else by_blocks[q])
+        first_rows = held.tile([P, HALF_BLOCKS, D], BF16, name="first_rows", align_bytes=ALIGNED)
+        nc.sync.dma_start(first_rows[:], table[:HALF, :].rearrange("(p b) d -> p b d", p=P))
+        rows = [first_rows[:, b, :] for b in range(HALF_BLOCKS)]
+        for begin in range(HALF, S, QUARTER):
+            last_rows = parts.tile([P, 2, D], BF16, name="last_rows", align_bytes=ALIGNED)
+            nc.sync.dma_start(
+                last_rows[:], table[begin : begin + QUARTER, :].rearrange("(e p) d -> p e d", p=P)
+            )
+            rows += [last_rows[:, e, :] for e in range(2)]
         targets = held.tile([D, M], BF16, name="targets", align_bytes=ALIGNED)
         nc.sync.dma_start(targets[:], w)
         offsets = held.tile([P, N // 16], U16, name="offsets", align_bytes=ALIGNED)
@@ -68,39 +71,35 @@ def tile_optimaltransportloss_kernel(tc, table, w, offs, out):
             )
 
         window = held.tile([D, S], BF16, name="window")
-        sums = [sums_and_scales.tile([P, 1], F32, name="sums") for b in range(2 * QUARTERS)]
-        for q in range(QUARTERS):
-            for e in range(2):
-                squares = unread_squares.tile([P, D], F32, name="squares")
-                block, total = rows[q][:, e, :], sums[2 * q + e][:]
-                if (q, e) in ((0, 0), (0, 1), (2, 0), (3, 0)):
-                    nc.scalar.activation(squares[:], block, SQUARE, accum_out=total)
-                else:
-                    nc.vector.scalar_tensor_tensor(
-                        squares[:], block, 1.0, block, op0=MULT, op1=MULT, accum_out=total
-                    )
-        scales = [sums_and_scales.tile([P, 1], F32, name="scales") for b in range(2 * QUARTERS)]
-        for b in range(2 * QUARTERS):
+        sums = [sums_and_scales.tile([P, 1], F32, name="sums") for b in range(BLOCKS)]
+        for b in range(BLOCKS):
+            squares = unread_squares.tile([P, D], F32, name="squares")
+            if b % 2 == 0:
+                nc.scalar.activation(squares[:], rows[b], SQUARE, accum_out=sums[b][:])
+            else:
+                nc.vector.scalar_tensor_tensor(
+                    squares[:], rows[b], 1.0, rows[b], op0=MULT, op1=MULT, accum_out=sums[b][:]
+                )
+        scales = [sums_and_scales.tile([P, 1], F32, name="scales") for b in range(BLOCKS)]
+        for b in range(BLOCKS):
             nc.scalar.activation(scales[b][:], sums[b][:], RSQRT)
         flipped = [
-            banks.tile([D, 2, P], BF16, name="flipped", tag="bank") for q in range(QUARTERS)
+            banks.tile([D, blocks, P], BF16, name="flipped", tag="bank")
+            for blocks in (HALF_BLOCKS, 2, 2)
         ]
-        for q in range(QUARTERS):
-            unit_rows = parts.tile([P, 2, D], BF16, name="unit_rows")
-            for e in range(2):
-                nc.vector.tensor_scalar(
-                    unit_rows[:, e, :], rows[q][:, e, :], scales[2 * q + e][:], None, op0=MULT
-                )
-                nc.tensor.transpose(flipped[q][:, e, :], unit_rows[:, e, :], identity[:])
-        for q in range(QUARTERS):
-            columns = window[:, q * QUARTER : (q + 1) * QUARTER]
-            if q < PAIRED:
-                nc.vector.tensor_copy(
-                    columns.rearrange("d (p e) -> d p e", e=2),
-                    flipped[q][:].rearrange("d e p -> d p e"),
-                )
-            else:
-                nc.vector.tensor_copy(columns, flipped[q][:].rearrange("d e p -> d (e p)"))
+        places = [bank[:, e, :] for bank in flipped for e in range(bank.shape[1])]
+        for b in range(BLOCKS):
+            unit_rows = unit.tile([P, D], BF16, name="unit_rows")
+            nc.vector.tensor_scalar(unit_rows[:], rows[b], scales[b][:], None, op0=MULT)
+            nc.tensor.transpose(places[b], unit_rows[:], identity[:])
+        nc.vector.tensor_copy(
+            window[:, :HALF].rearrange("d (p b) -> d p b", p=P),
+            flipped[0][:].rearrange("d b p -> d p b"),
+        )
+        for bank, begin in zip(flipped[1:], range(HALF, S, QUARTER)):
+            nc.vector.tensor_copy(
+                window[:, begin : begin + QUARTER], bank[:].rearrange("d e p -> d (e p)")
+            )
 
         target_sums = held.tile([P, M_BLOCKS], F32, name="target_sums")
         for mb in range(M_BLOCKS):

import concourse.mybir as mybir
from concourse.masks import make_identity

BF16, F32, U16 = mybir.dt.bfloat16, mybir.dt.float32, mybir.dt.uint16
MULT, ADD = mybir.AluOpType.mult, mybir.AluOpType.add
RSQRT = mybir.ActivationFunctionType.Abs_reciprocal_sqrt
SQUARE = mybir.ActivationFunctionType.Square
COPY = mybir.ActivationFunctionType.Copy

P = 128
S, D, M, N = 1024, 128, 512, 1024
BLOCKS = S // P
HALF, QUARTER = S // 2, S // 4
HALF_BLOCKS = HALF // P
M_BLOCKS = M // P
BANK = 512
PIECE = 256
PIECES = N // PIECE
PIECE_COLUMNS = PIECE // 16

WARM_BEFORE = 4

ALIGNED = 1024

FLOPS = 2 * M * N * D


def tile_optimaltransportloss_kernel(tc, table, w, offs, out):
    nc = tc.nc
    with (
        tc.tile_pool(name="held", bufs=1) as held,
        tc.tile_pool(name="parts", bufs=M_BLOCKS) as parts,
        tc.tile_pool(name="unread_squares", bufs=BLOCKS) as unread_squares,
        tc.tile_pool(name="sums_and_scales", bufs=BLOCKS) as sums_and_scales,
        tc.tile_pool(name="unit", bufs=BLOCKS) as unit,
        tc.tile_pool(name="staged", bufs=M_BLOCKS * PIECES + 2) as staged,
        tc.psum_pool(name="once", bufs=1) as once,
        tc.psum_pool(name="banks", bufs=6) as banks,
    ):
        first_rows = held.tile([P, HALF_BLOCKS, D], BF16, name="first_rows", align_bytes=ALIGNED)
        nc.sync.dma_start(first_rows[:], table[:HALF, :].rearrange("(p b) d -> p b d", p=P))
        rows = [first_rows[:, b, :] for b in range(HALF_BLOCKS)]
        for begin in range(HALF, S, QUARTER):
            last_rows = parts.tile([P, 2, D], BF16, name="last_rows", align_bytes=ALIGNED)
            nc.sync.dma_start(
                last_rows[:], table[begin : begin + QUARTER, :].rearrange("(e p) d -> p e d", p=P)
            )
            rows += [last_rows[:, e, :] for e in range(2)]
        targets = held.tile([D, M], BF16, name="targets", align_bytes=ALIGNED)
        nc.sync.dma_start(targets[:], w)
        offsets = held.tile([P, N // 16], U16, name="offsets", align_bytes=ALIGNED)
        nc.sync.dma_start(offsets[:], offs)

        unity = held.tile([P, 1], F32, name="unity")
        nc.gpsimd.memset(unity[:], 1.0)
        nc.scalar.activation(unity[:], unity[:], RSQRT)

        identity = held.tile([P, P], BF16, name="identity")
        make_identity(nc, identity[:])

        zeros = held.tile([P, BANK], BF16, name="zeros")
        nc.vector.memset(zeros[:], 0.0)
        unread = once.tile([P, BANK], F32, name="unread")
        for turn in range(WARM_BEFORE):
            nc.tensor.matmul(unread[:], zeros[:, :P], zeros[:], start=True, stop=True)

        flipped_targets = once.tile([P, M_BLOCKS, D], BF16, name="flipped_targets")
        for mb in range(M_BLOCKS):
            nc.tensor.transpose(
                flipped_targets[:, mb, :], targets[:, mb * P : (mb + 1) * P], identity[:]
            )

        window = held.tile([D, S], BF16, name="window")
        sums = [sums_and_scales.tile([P, 1], F32, name="sums") for b in range(BLOCKS)]
        for b in range(BLOCKS):
            squares = unread_squares.tile([P, D], F32, name="squares")
            if b % 2 == 0:
                nc.scalar.activation(squares[:], rows[b], SQUARE, accum_out=sums[b][:])
            else:
                nc.vector.scalar_tensor_tensor(
                    squares[:], rows[b], 1.0, rows[b], op0=MULT, op1=MULT, accum_out=sums[b][:]
                )
        scales = [sums_and_scales.tile([P, 1], F32, name="scales") for b in range(BLOCKS)]
        for b in range(BLOCKS):
            nc.scalar.activation(scales[b][:], sums[b][:], RSQRT)
        flipped = [
            banks.tile([D, blocks, P], BF16, name="flipped", tag="bank")
            for blocks in (HALF_BLOCKS, 2, 2)
        ]
        places = [bank[:, e, :] for bank in flipped for e in range(bank.shape[1])]
        for b in range(BLOCKS):
            unit_rows = unit.tile([P, D], BF16, name="unit_rows")
            nc.vector.tensor_scalar(unit_rows[:], rows[b], scales[b][:], None, op0=MULT)
            nc.tensor.transpose(places[b], unit_rows[:], identity[:])
        nc.vector.tensor_copy(
            window[:, :HALF].rearrange("d (p b) -> d p b", p=P),
            flipped[0][:].rearrange("d b p -> d p b"),
        )
        for bank, begin in zip(flipped[1:], range(HALF, S, QUARTER)):
            nc.vector.tensor_copy(
                window[:, begin : begin + QUARTER], bank[:].rearrange("d e p -> d (e p)")
            )

        target_sums = held.tile([P, M_BLOCKS], F32, name="target_sums")
        for mb in range(M_BLOCKS):
            target_squares = parts.tile([P, D], F32, name="target_squares")
            nc.scalar.activation(
                target_squares[:],
                flipped_targets[:, mb, :],
                SQUARE,
                accum_out=target_sums[:, mb : mb + 1],
            )
        target_scales = held.tile([P, M_BLOCKS], F32, name="target_scales")
        nc.scalar.activation(target_scales[:], target_sums[:], RSQRT)
        minus_scales = held.tile([P, M_BLOCKS], F32, name="minus_scales")
        nc.scalar.mul(minus_scales[:], target_scales[:], -1.0)

        for mb in range(M_BLOCKS):
            minus_scale = minus_scales[:, mb : mb + 1]
            for piece in range(PIECES):
                looked_up = window[:].indirect(
                    offsets[:, piece * PIECE_COLUMNS : (piece + 1) * PIECE_COLUMNS]
                )
                product = banks.tile([P, PIECE], F32, name="product", tag="bank")
                nc.tensor.matmul(
                    product[:], targets[:, mb * P : (mb + 1) * P], looked_up, start=True, stop=True
                )
                outermost = (mb, piece) in ((0, 0), (M_BLOCKS - 1, PIECES - 1))
                columns = PIECE // 2 if outermost else PIECE
                for begin in range(0, PIECE, columns):
                    distance = staged.tile([P, columns], F32, name="distance", align_bytes=ALIGNED)
                    if piece % 2 == 0:
                        nc.vector.tensor_scalar(
                            distance[:],
                            product[:, begin : begin + columns],
                            minus_scale,
                            1.0,
                            op0=MULT,
                            op1=ADD,
                        )
                    else:
                        nc.scalar.activation(
                            distance[:],
                            product[:, begin : begin + columns],
                            COPY,
                            bias=1.0,
                            scale=minus_scale,
                        )
                    nc.sync.dma_start(
                        out[
                            mb * P : (mb + 1) * P,
                            piece * PIECE + begin : piece * PIECE + begin + columns,
                        ],
                        distance[:],
                    )
